import numpy as np
import ml_dtypes


def mxq(x, axis, fmt="e4m3"):
    dtype, down = {"e4m3": (ml_dtypes.float8_e4m3fn, 7), "e5m2": (ml_dtypes.float8_e5m2, 14)}[fmt]
    v = np.moveaxis(np.asarray(x, np.float32).astype(ml_dtypes.bfloat16).astype(np.float64), axis, -1)
    blocks = v.reshape(v.shape[:-1] + (-1, 32))
    amax = np.abs(blocks).max(-1, keepdims=True)
    byte = np.maximum(np.where(amax > 0, np.frexp(amax)[1] - 1 + 127, 0) - down, 1)
    scale = np.exp2(byte - 127.0)
    codes = (blocks / scale).astype(np.float32).astype(dtype).astype(np.float64)
    return np.moveaxis((codes * scale).reshape(v.shape), -1, axis)


WIDE = False


def mx_kscale(k):
    if not WIDE:
        return np.ones(k)
    levels = np.array([10, -10, 5, -5, 0])
    a = np.random.permutation(np.resize(levels, k // 512 * 4)).reshape(k // 512, 4)
    idx = np.arange(k)
    return np.exp2(a[idx // 512, idx % 128 // 32])


BF16 = ml_dtypes.bfloat16


def bf(x):
    return np.asarray(x, np.float32).astype(BF16)


def f64(x):
    return np.asarray(x).astype(np.float64)


B, T, D, H, DH, F = 4, 1024, 1024, 4, 64, 4096
A = H * DH
EPS = 1e-6


def layer_norm(v, gain, bias):
    mu = v.mean(-1, keepdims=True)
    var = np.square(v - mu).mean(-1, keepdims=True)
    return (v - mu) * (1.0 / np.sqrt(var + EPS)) * gain + bias


def setup_inputs():
    s = mx_kscale(D)
    r = np.random.standard_normal
    return {"x": bf(r((B, T, D))),
            "ln1_gain": bf((1.0 + 0.1 * r(D)) * s),
            "ln1_bias": bf(0.1 * r(D) * s),
            "wq": bf(r((D, A)) / np.sqrt(D) / s[:, None]),
            "bq": bf(0.1 * r(A)),
            "wk": bf(r((D, A)) / np.sqrt(D) / s[:, None]),
            "bk": bf(0.1 * r(A)),
            "wv": bf(r((D, A)) / np.sqrt(D) / s[:, None]),
            "bv": bf(0.1 * r(A))}


def reference(x, ln1_gain, ln1_bias, wq, bq, wk, bk, wv, bv):
    h = layer_norm(f64(x), f64(ln1_gain), f64(ln1_bias))
    hq = mxq(h, 2, "e4m3")
    q = ((hq @ mxq(f64(wq), 0, "e4m3")) + f64(bq)).reshape(B, T, H, DH)
    k = ((hq @ mxq(f64(wk), 0, "e4m3")) + f64(bk)).reshape(B, T, H, DH)
    v = ((hq @ mxq(f64(wv), 0, "e4m3")) + f64(bv)).reshape(B, T, H, DH)
    return q, k, v

@@ -1,0 +1,248 @@
+from contextlib import ExitStack
+
+import concourse.mybir as mybir
+from concourse.masks import make_identity
+
+F32 = mybir.dt.float32
+BF16 = mybir.dt.bfloat16
+U32 = mybir.dt.uint32
+U8 = mybir.dt.uint8
+FP8X4 = mybir.dt.float8_e4m3fn_x4
+ALU = mybir.AluOpType
+ACT = mybir.ActivationFunctionType
+
+P = 128
+PACK = 4
+K_PASS = P * PACK
+TOKENS = 4 * 1024
+D = 1024
+C = 256
+EPS = 1e-6
+
+PASSES = D // K_PASS
+K_TILES = D // P
+A = 4
+GROUP = A * P
+GROUPS = TOKENS // GROUP
+BN_MAX = 512
+QK = slice(0, 2 * C)
+V = slice(2 * C, 3 * C)
+
+FLOPS = 2 * TOKENS * D * 3 * C
+
+
+def tile_swidtblock_pa_t_kernel(
+    tc, x, ln1_gain, ln1_bias, wq, bq, wk, bk, wv, bv, out_0, out_1, out_2
+):
+    nc = tc.nc
+    x_groups = x.flatten_outer_dims().rearrange("(s p a) d -> s p a d", p=P, a=A)
+    out_groups = [
+        o.rearrange("b t h e -> (b t) (h e)").rearrange("(s p a) c -> s p a c", p=P, a=A)
+        for o in (out_0, out_1, out_2)
+    ]
+
+    with ExitStack() as ctx:
+        const = ctx.enter_context(tc.tile_pool(name="const", bufs=1))
+        xpool = ctx.enter_context(tc.tile_pool(name="xpool", bufs=GROUPS))
+        small = ctx.enter_context(tc.tile_pool(name="small", bufs=4))
+        work = ctx.enter_context(tc.tile_pool(name="work", bufs=2))
+        opool = ctx.enter_context(tc.tile_pool(name="opool", bufs=3))
+        psum_t = ctx.enter_context(tc.psum_pool(name="psum_t", bufs=4))
+        psum_o = ctx.enter_context(tc.psum_pool(name="psum_o", bufs=2))
+
+        x_tiles = []
+
+        def load_x(s):
+            x_sb = xpool.tile([P, A, D], BF16)
+            nc.sync.dma_start(out=x_sb[:], in_=x_groups[s])
+            x_tiles.append(x_sb)
+
+        load_x(0)
+        w_raw = const.tile([P, 3, PASSES, PACK, C], BF16)
+        for o, w in enumerate((wq, wk, wv)):
+            nc.sync.dma_start(
+                out=w_raw[:, o], in_=w.rearrange("(g j p) c -> p g j c", j=PACK, p=P)
+            )
+        for s in range(1, GROUPS):
+            load_x(s)
+
+        ident = const.tile([P, P], F32)
+        make_identity(nc, ident[:])
+        eps = const.tile([P, 1], F32)
+        nc.vector.memset(eps[:], EPS)
+
+        ln_rows = const.tile([P, P], BF16)
+        nc.vector.memset(ln_rows[:], 0.0)
+        nc.scalar.dma_start(out=ln_rows[0:K_TILES, :], in_=ln1_gain.rearrange("(r c) -> r c", c=P))
+        nc.scalar.dma_start(
+            out=ln_rows[K_TILES : 2 * K_TILES, :], in_=ln1_bias.rearrange("(r c) -> r c", c=P)
+        )
+        ln_rows_f32 = const.tile([P, P], F32)
+        nc.vector.tensor_copy(out=ln_rows_f32[:], in_=ln_rows[:])
+        ln_cols_ps = psum_t.tile([P, P], F32, tag="bank")
+        nc.tensor.transpose(ln_cols_ps[:], ln_rows_f32[:], ident[:])
+        ln_cols = const.tile([P, 2 * K_TILES], F32)
+        nc.vector.tensor_copy(out=ln_cols[:], in_=ln_cols_ps[:, 0 : 2 * K_TILES])
+
+        bias_rows = const.tile([P, 3 * C], BF16)
+        nc.vector.memset(bias_rows[:], 0.0)
+        for o, b in enumerate((bq, bk, bv)):
+            nc.scalar.dma_start(
+                out=bias_rows[0:1, o * C : (o + 1) * C], in_=b.rearrange("(r c) -> r c", r=1)
+            )
+        ones = const.tile([P, P], BF16)
+        nc.vector.memset(ones[:], 1.0)
+        out_bias = const.tile([P, 3 * C], F32)
+        for cols, width in ((QK, 2 * C), (V, C)):
+            bias_ps = psum_t.tile([P, 2 * C], F32, tag="bank")
+            nc.tensor.matmul(
+                bias_ps[:, 0:width], lhsT=ones[:], rhs=bias_rows[:, cols], start=True, stop=True
+            )
+            nc.vector.tensor_copy(out=out_bias[:, cols], in_=bias_ps[:, 0:width])
+
+        w_grouped = const.tile([P, PASSES, 3 * C, PACK], BF16, align_bytes=64)
+        w_codes = const.tile([P, PASSES, 3 * C], U32, align_bytes=64)
+        w_scales = const.tile([P, PASSES, 3 * C], U8, align_bytes=64)
+
+        def regroup_weights():
+            for o in range(3):
+                for g in range(PASSES):
+                    dst = w_grouped[:, g, o * C : (o + 1) * C, :]
+                    src = w_raw[:, o, g].rearrange("p j c -> p c j")
+                    if g % 2 == 0:
+                        nc.scalar.copy(out=dst, in_=src)
+                    else:
+                        nc.gpsimd.tensor_scalar(
+                            out=dst, in0=src, scalar1=1.0, scalar2=0.0, op0=ALU.mult, op1=ALU.add
+                        )
+
+        def quantise_weights():
+            for g in range(PASSES):
+                for cols in (QK, V):
+                    nc.vector.quantize_mx(
+                        out=w_codes[:, g, cols].bitcast(FP8X4),
+                        scales=w_scales[:, g, cols],
+                        in_=w_grouped[:, g, cols, :].rearrange("p c j -> p (c j)"),
+                    )
+
+        n_tiles = {}
+        h_codes = {}
+        h_scales = {}
+        grouped_tiles = {}
+
+        def normalise(s):
+            x_sb = x_tiles[s]
+            stats = small.tile([P, A, D // BN_MAX, 6], F32)
+            mean_var = small.tile([P, A, 2], F32)
+            for a in range(A):
+                for half in range(D // BN_MAX):
+                    nc.vector.bn_stats(
+                        out=stats[:, a, half, :],
+                        in_=x_sb[:, a, half * BN_MAX : (half + 1) * BN_MAX],
+                    )
+                nc.vector.bn_aggr(
+                    out=mean_var[:, a, :], in_=stats[:, a].rearrange("p h s -> p (h s)")
+                )
+            std = small.tile([P, A], F32)
+            nc.scalar.activation(
+                out=std[:], in_=mean_var[:, :, 1], func=ACT.Sqrt, bias=eps[:, 0:1], scale=1.0
+            )
+            rstd = small.tile([P, A], F32)
+            nc.vector.reciprocal(out=rstd[:], in_=std[:])
+            shift = small.tile([P, A], F32)
+            nc.vector.scalar_tensor_tensor(
+                out=shift[:], in0=mean_var[:, :, 0], scalar=-1.0, in1=rstd[:],
+                op0=ALU.mult, op1=ALU.mult,
+            )
+            n_sb = work.tile([P, A, D], F32)
+            for a in range(A):
+                if a % 2 == 0:
+                    nc.scalar.activation(
+                        out=n_sb[:, a, :], in_=x_sb[:, a, :], func=ACT.Identity,
+                        scale=rstd[:, a : a + 1], bias=shift[:, a : a + 1],
+                    )
+                else:
+                    nc.gpsimd.tensor_scalar(
+                        out=n_sb[:, a, :], in0=x_sb[:, a, :],
+                        scalar1=rstd[:, a : a + 1], scalar2=shift[:, a : a + 1],
+                        op0=ALU.mult, op1=ALU.add,
+                    )
+            n_tiles[s] = n_sb
+
+        def transpose_and_scale(s):
+            n_sb = n_tiles[s]
+            h_t = work.tile([P, K_TILES, GROUP], BF16)
+            grouped = work.tile([P, PASSES, GROUP, PACK], BF16, align_bytes=64)
+            for t in range(K_TILES):
+                bank = psum_t.tile([P, GROUP], F32, tag="bank")
+                for a in range(A):
+                    nc.tensor.transpose(
+                        bank[:, a * P : (a + 1) * P], n_sb[:, a, t * P : (t + 1) * P], ident[:]
+                    )
+                nc.scalar.activation(
+                    out=h_t[:, t, :], in_=bank[:], func=ACT.Identity,
+                    scale=ln_cols[:, t : t + 1], bias=ln_cols[:, K_TILES + t : K_TILES + t + 1],
+                )
+            for g in range(PASSES):
+                nc.gpsimd.tensor_scalar(
+                    out=grouped[:, g],
+                    in0=h_t[:, g * PACK : (g + 1) * PACK, :].rearrange("p j c -> p c j"),
+                    scalar1=1.0, scalar2=0.0, op0=ALU.mult, op1=ALU.add,
+                )
+            grouped_tiles[s] = grouped
+
+        def quantise(s):
+            grouped = grouped_tiles[s]
+            codes = work.tile([P, PASSES, GROUP], U32, align_bytes=64)
+            scales = work.tile([P, PASSES, GROUP], U8, align_bytes=64)
+            for g in range(PASSES):
+                nc.vector.quantize_mx(
+                    out=codes[:, g, :].bitcast(FP8X4),
+                    scales=scales[:, g, :],
+                    in_=grouped[:, g].rearrange("p c j -> p (c j)"),
+                )
+            h_codes[s] = codes
+            h_scales[s] = scales
+
+        def project(s):
+            codes = h_codes[s]
+            scales = h_scales[s]
+            result = opool.tile([P, 3, A, C], F32)
+            for a in range(A):
+                tokens = slice(a * P, (a + 1) * P)
+                acc_qk = psum_o.tile([P, 2 * C], F32)
+                acc_v = psum_o.tile([P, C], F32)
+                for g in range(PASSES):
+                    for acc, cols in ((acc_qk, QK), (acc_v, V)):
+                        nc.tensor.matmul_mx(
+                            out=acc[:],
+                            lhsT=codes[:, g, tokens].bitcast(FP8X4),
+                            lhsT_scale=scales[:, g, tokens],
+                            rhs=w_codes[:, g, cols].bitcast(FP8X4),
+                            rhs_scale=w_scales[:, g, cols],
+                            start=(g == 0),
+                            stop=(g == PASSES - 1),
+                        )
+                nc.vector.tensor_tensor(
+                    out=result[:, 0:2, a, :],
+                    in0=acc_qk[:].rearrange("p (o c) -> p o c", o=2),
+                    in1=out_bias[:, QK].rearrange("p (o c) -> p o c", o=2),
+                    op=ALU.add,
+                )
+                nc.vector.tensor_tensor(
+                    out=result[:, 2, a, :], in0=acc_v[:], in1=out_bias[:, V], op=ALU.add
+                )
+            for o in range(3):
+                nc.sync.dma_start(out=out_groups[o][s], in_=result[:, o])
+
+        regroup_weights()
+        for step in range(GROUPS + 2):
+            if step < GROUPS:
+                normalise(step)
+            if step == 0:
+                quantise_weights()
+            if 1 <= step <= GROUPS:
+                transpose_and_scale(step - 1)
+            if step >= 2:
+                quantise(step - 2)
+                project(step - 2)

@@ -49,6 +49,7 @@ def tile_swidtblock_pa_t_kernel(
         opool = ctx.enter_context(tc.tile_pool(name="opool", bufs=3))
         psum_t = ctx.enter_context(tc.psum_pool(name="psum_t", bufs=4))
         psum_o = ctx.enter_context(tc.psum_pool(name="psum_o", bufs=2))
+        ctx.enter_context(tc.manual_schedule())
 
         x_tiles = []
 
@@ -70,6 +71,8 @@ def tile_swidtblock_pa_t_kernel(
         make_identity(nc, ident[:])
         eps = const.tile([P, 1], F32)
         nc.vector.memset(eps[:], EPS)
+        ones = const.tile([P, P], BF16)
+        nc.vector.memset(ones[:], 1.0)
 
         ln_rows = const.tile([P, P], BF16)
         nc.vector.memset(ln_rows[:], 0.0)
@@ -77,28 +80,27 @@ def tile_swidtblock_pa_t_kernel(
         nc.scalar.dma_start(
             out=ln_rows[K_TILES : 2 * K_TILES, :], in_=ln1_bias.rearrange("(r c) -> r c", c=P)
         )
-        ln_rows_f32 = const.tile([P, P], F32)
-        nc.vector.tensor_copy(out=ln_rows_f32[:], in_=ln_rows[:])
-        ln_cols_ps = psum_t.tile([P, P], F32, tag="bank")
-        nc.tensor.transpose(ln_cols_ps[:], ln_rows_f32[:], ident[:])
-        ln_cols = const.tile([P, 2 * K_TILES], F32)
-        nc.vector.tensor_copy(out=ln_cols[:], in_=ln_cols_ps[:, 0 : 2 * K_TILES])
-
         bias_rows = const.tile([P, 3 * C], BF16)
         nc.vector.memset(bias_rows[:], 0.0)
         for o, b in enumerate((bq, bk, bv)):
             nc.scalar.dma_start(
                 out=bias_rows[0:1, o * C : (o + 1) * C], in_=b.rearrange("(r c) -> r c", r=1)
             )
-        ones = const.tile([P, P], BF16)
-        nc.vector.memset(ones[:], 1.0)
+        ln_cols = const.tile([P, 2 * K_TILES], F32)
         out_bias = const.tile([P, 3 * C], F32)
-        for cols, width in ((QK, 2 * C), (V, C)):
-            bias_ps = psum_t.tile([P, 2 * C], F32, tag="bank")
-            nc.tensor.matmul(
-                bias_ps[:, 0:width], lhsT=ones[:], rhs=bias_rows[:, cols], start=True, stop=True
-            )
-            nc.vector.tensor_copy(out=out_bias[:, cols], in_=bias_ps[:, 0:width])
+
+        def spread_vectors():
+            ln_rows_f32 = const.tile([P, P], F32)
+            nc.vector.tensor_copy(out=ln_rows_f32[:], in_=ln_rows[:])
+            ln_cols_ps = psum_t.tile([P, P], F32, tag="bank")
+            nc.tensor.transpose(ln_cols_ps[:], ln_rows_f32[:], ident[:])
+            nc.vector.tensor_copy(out=ln_cols[:], in_=ln_cols_ps[:, 0 : 2 * K_TILES])
+            for cols, width in ((QK, 2 * C), (V, C)):
+                bias_ps = psum_t.tile([P, 2 * C], F32, tag="bank")
+                nc.tensor.matmul(
+                    bias_ps[:, 0:width], lhsT=ones[:], rhs=bias_rows[:, cols], start=True, stop=True
+                )
+                nc.vector.tensor_copy(out=out_bias[:, cols], in_=bias_ps[:, 0:width])
 
         w_grouped = const.tile([P, PASSES, 3 * C, PACK], BF16, align_bytes=64)
         w_codes = const.tile([P, PASSES, 3 * C], U32, align_bytes=64)
@@ -125,24 +127,30 @@ def tile_swidtblock_pa_t_kernel(
                         in_=w_grouped[:, g, cols, :].rearrange("p c j -> p (c j)"),
                     )
 
+        stat_tiles = {}
         n_tiles = {}
-        h_codes = {}
-        h_scales = {}
-        grouped_tiles = {}
+        h_tiles = {}
+        code_tiles = {}
+        result_tiles = {}
 
-        def normalise(s):
-            x_sb = x_tiles[s]
-            stats = small.tile([P, A, D // BN_MAX, 6], F32)
-            mean_var = small.tile([P, A, 2], F32)
-            for a in range(A):
+        def statistics(s, tiles):
+            if s not in stat_tiles:
+                stats = small.tile([P, A, D // BN_MAX, 6], F32)
+                mean_var = small.tile([P, A, 2], F32)
+                stat_tiles[s] = (stats, mean_var)
+            stats, mean_var = stat_tiles[s]
+            for a in tiles:
                 for half in range(D // BN_MAX):
                     nc.vector.bn_stats(
                         out=stats[:, a, half, :],
-                        in_=x_sb[:, a, half * BN_MAX : (half + 1) * BN_MAX],
+                        in_=x_tiles[s][:, a, half * BN_MAX : (half + 1) * BN_MAX],
                     )
                 nc.vector.bn_aggr(
                     out=mean_var[:, a, :], in_=stats[:, a].rearrange("p h s -> p (h s)")
                 )
+
+        def scale_and_shift(s):
+            mean_var = stat_tiles[s][1]
             std = small.tile([P, A], F32)
             nc.scalar.activation(
                 out=std[:], in_=mean_var[:, :, 1], func=ACT.Sqrt, bias=eps[:, 0:1], scale=1.0
@@ -155,25 +163,33 @@ def tile_swidtblock_pa_t_kernel(
                 op0=ALU.mult, op1=ALU.mult,
             )
             n_sb = work.tile([P, A, D], F32)
-            for a in range(A):
-                if a % 2 == 0:
-                    nc.scalar.activation(
-                        out=n_sb[:, a, :], in_=x_sb[:, a, :], func=ACT.Identity,
-                        scale=rstd[:, a : a + 1], bias=shift[:, a : a + 1],
-                    )
-                else:
-                    nc.gpsimd.tensor_scalar(
-                        out=n_sb[:, a, :], in0=x_sb[:, a, :],
-                        scalar1=rstd[:, a : a + 1], scalar2=shift[:, a : a + 1],
-                        op0=ALU.mult, op1=ALU.add,
-                    )
-            n_tiles[s] = n_sb
+            n_tiles[s] = (n_sb, rstd, shift)
 
-        def transpose_and_scale(s):
-            n_sb = n_tiles[s]
-            h_t = work.tile([P, K_TILES, GROUP], BF16)
-            grouped = work.tile([P, PASSES, GROUP, PACK], BF16, align_bytes=64)
-            for t in range(K_TILES):
+        def normalise_on_gpsimd(s, tiles):
+            n_sb, rstd, shift = n_tiles[s]
+            for a in tiles:
+                nc.gpsimd.tensor_scalar(
+                    out=n_sb[:, a, :], in0=x_tiles[s][:, a, :],
+                    scalar1=rstd[:, a : a + 1], scalar2=shift[:, a : a + 1],
+                    op0=ALU.mult, op1=ALU.add,
+                )
+
+        def normalise_on_scalar(s, tiles):
+            n_sb, rstd, shift = n_tiles[s]
+            for a in tiles:
+                nc.scalar.activation(
+                    out=n_sb[:, a, :], in_=x_tiles[s][:, a, :], func=ACT.Identity,
+                    scale=rstd[:, a : a + 1], bias=shift[:, a : a + 1],
+                )
+
+        def transpose_and_scale(s, g):
+            n_sb = n_tiles[s][0]
+            if s not in h_tiles:
+                h_t = work.tile([P, K_TILES, GROUP], BF16)
+                grouped = work.tile([P, PASSES, GROUP, PACK], BF16, align_bytes=64)
+                h_tiles[s] = (h_t, grouped)
+            h_t, grouped = h_tiles[s]
+            for t in range(g * PACK, (g + 1) * PACK):
                 bank = psum_t.tile([P, GROUP], F32, tag="bank")
                 for a in range(A):
                     nc.tensor.transpose(
@@ -183,16 +199,14 @@ def tile_swidtblock_pa_t_kernel(
                     out=h_t[:, t, :], in_=bank[:], func=ACT.Identity,
                     scale=ln_cols[:, t : t + 1], bias=ln_cols[:, K_TILES + t : K_TILES + t + 1],
                 )
-            for g in range(PASSES):
-                nc.gpsimd.tensor_scalar(
-                    out=grouped[:, g],
-                    in0=h_t[:, g * PACK : (g + 1) * PACK, :].rearrange("p j c -> p c j"),
-                    scalar1=1.0, scalar2=0.0, op0=ALU.mult, op1=ALU.add,
-                )
-            grouped_tiles[s] = grouped
+            nc.gpsimd.tensor_scalar(
+                out=grouped[:, g],
+                in0=h_t[:, g * PACK : (g + 1) * PACK, :].rearrange("p j c -> p c j"),
+                scalar1=1.0, scalar2=0.0, op0=ALU.mult, op1=ALU.add,
+            )
 
         def quantise(s):
-            grouped = grouped_tiles[s]
+            grouped = h_tiles[s][1]
             codes = work.tile([P, PASSES, GROUP], U32, align_bytes=64)
             scales = work.tile([P, PASSES, GROUP], U8, align_bytes=64)
             for g in range(PASSES):
@@ -201,17 +215,20 @@ def tile_swidtblock_pa_t_kernel(
                     scales=scales[:, g, :],
                     in_=grouped[:, g].rearrange("p c j -> p (c j)"),
                 )
-            h_codes[s] = codes
-            h_scales[s] = scales
+            code_tiles[s] = (codes, scales)
 
-        def project(s):
-            codes = h_codes[s]
-            scales = h_scales[s]
-            result = opool.tile([P, 3, A, C], F32)
-            for a in range(A):
+        def project(s, tiles):
+            codes, scales = code_tiles[s]
+            if s not in result_tiles:
+                result = opool.tile([P, 3, A, C], F32)
+                result_tiles[s] = result
+            result = result_tiles[s]
+            accs = {}
+            for a in tiles:
                 tokens = slice(a * P, (a + 1) * P)
                 acc_qk = psum_o.tile([P, 2 * C], F32)
                 acc_v = psum_o.tile([P, C], F32)
+                accs[a] = (acc_qk, acc_v)
                 for g in range(PASSES):
                     for acc, cols in ((acc_qk, QK), (acc_v, V)):
                         nc.tensor.matmul_mx(
@@ -223,6 +240,8 @@ def tile_swidtblock_pa_t_kernel(
                             start=(g == 0),
                             stop=(g == PASSES - 1),
                         )
+            for a in tiles:
+                acc_qk, acc_v = accs[a]
                 nc.vector.tensor_tensor(
                     out=result[:, 0:2, a, :],
                     in0=acc_qk[:].rearrange("p (o c) -> p o c", o=2),
@@ -232,17 +251,31 @@ def tile_swidtblock_pa_t_kernel(
                 nc.vector.tensor_tensor(
                     out=result[:, 2, a, :], in0=acc_v[:], in1=out_bias[:, V], op=ALU.add
                 )
+
+        def store(s):
             for o in range(3):
-                nc.sync.dma_start(out=out_groups[o][s], in_=result[:, o])
+                nc.sync.dma_start(out=out_groups[o][s], in_=result_tiles[s][:, o])
 
         regroup_weights()
-        for step in range(GROUPS + 2):
-            if step < GROUPS:
-                normalise(step)
-            if step == 0:
+        for r in range(GROUPS + 3):
+            if r == 1:
+                spread_vectors()
+            if r == 2:
                 quantise_weights()
-            if 1 <= step <= GROUPS:
-                transpose_and_scale(step - 1)
-            if step >= 2:
-                quantise(step - 2)
-                project(step - 2)
+            if r >= 3:
+                quantise(r - 3)
+            if 1 <= r <= GROUPS:
+                normalise_on_gpsimd(r - 1, (1, 3))
+            for half in range(2):
+                if 2 <= r <= GROUPS + 1:
+                    transpose_and_scale(r - 2, half)
+                if r < GROUPS:
+                    statistics(r, (2 * half, 2 * half + 1))
+                if r >= 3:
+                    project(r - 3, (2 * half, 2 * half + 1))
+            if r >= 3:
+                store(r - 3)
+            if 1 <= r <= GROUPS:
+                normalise_on_scalar(r - 1, (0, 2))
+            if r < GROUPS:
+                scale_and_shift(r)

@@ -25,8 +25,15 @@ A = 4
 GROUP = A * P
 GROUPS = TOKENS // GROUP
 BN_MAX = 512
+BANK = 512
 QK = slice(0, 2 * C)
 V = slice(2 * C, 3 * C)
+
+STEPS = 2 * GROUPS
+LAG_TRANSPOSE = 5
+LAG_QUANTISE = 8
+LAG_MULTIPLY = 9
+LAG_OUT = 10
 
 FLOPS = 2 * TOKENS * D * 3 * C
 
@@ -45,10 +52,9 @@ def tile_swidtblock_pa_t_kernel(
         const = ctx.enter_context(tc.tile_pool(name="const", bufs=1))
         xpool = ctx.enter_context(tc.tile_pool(name="xpool", bufs=GROUPS))
         small = ctx.enter_context(tc.tile_pool(name="small", bufs=4))
-        work = ctx.enter_context(tc.tile_pool(name="work", bufs=2))
-        opool = ctx.enter_context(tc.tile_pool(name="opool", bufs=3))
-        psum_t = ctx.enter_context(tc.psum_pool(name="psum_t", bufs=4))
-        psum_o = ctx.enter_context(tc.psum_pool(name="psum_o", bufs=2))
+        work2 = ctx.enter_context(tc.tile_pool(name="work2", bufs=2))
+        work3 = ctx.enter_context(tc.tile_pool(name="work3", bufs=3))
+        psum = ctx.enter_context(tc.psum_pool(name="psum", bufs=8))
         ctx.enter_context(tc.manual_schedule())
 
         x_tiles = []
@@ -88,19 +94,25 @@ def tile_swidtblock_pa_t_kernel(
             )
         ln_cols = const.tile([P, 2 * K_TILES], F32)
         out_bias = const.tile([P, 3 * C], F32)
+        spread = {}
 
         def spread_vectors():
             ln_rows_f32 = const.tile([P, P], F32)
             nc.vector.tensor_copy(out=ln_rows_f32[:], in_=ln_rows[:])
-            ln_cols_ps = psum_t.tile([P, P], F32, tag="bank")
-            nc.tensor.transpose(ln_cols_ps[:], ln_rows_f32[:], ident[:])
-            nc.vector.tensor_copy(out=ln_cols[:], in_=ln_cols_ps[:, 0 : 2 * K_TILES])
-            for cols, width in ((QK, 2 * C), (V, C)):
-                bias_ps = psum_t.tile([P, 2 * C], F32, tag="bank")
+            ln_cols_ps = psum.tile([P, BANK], F32, tag="bank")
+            nc.tensor.transpose(ln_cols_ps[:, 0:P], ln_rows_f32[:], ident[:])
+            spread["ln"] = ln_cols_ps
+            for name, cols, width in (("qk", QK, 2 * C), ("v", V, C)):
+                bias_ps = psum.tile([P, BANK], F32, tag="bank")
                 nc.tensor.matmul(
                     bias_ps[:, 0:width], lhsT=ones[:], rhs=bias_rows[:, cols], start=True, stop=True
                 )
-                nc.vector.tensor_copy(out=out_bias[:, cols], in_=bias_ps[:, 0:width])
+                spread[name] = bias_ps
+
+        def keep_spread_vectors():
+            nc.vector.tensor_copy(out=ln_cols[:], in_=spread["ln"][:, 0 : 2 * K_TILES])
+            nc.vector.tensor_copy(out=out_bias[:, QK], in_=spread["qk"][:, 0 : 2 * C])
+            nc.vector.tensor_copy(out=out_bias[:, V], in_=spread["v"][:, 0:C])
 
         w_grouped = const.tile([P, PASSES, 3 * C, PACK], BF16, align_bytes=64)
         w_codes = const.tile([P, PASSES, 3 * C], U32, align_bytes=64)
@@ -131,6 +143,7 @@ def tile_swidtblock_pa_t_kernel(
         n_tiles = {}
         h_tiles = {}
         code_tiles = {}
+        acc_tiles = {}
         result_tiles = {}
 
         def statistics(s, tiles):
@@ -145,16 +158,21 @@ def tile_swidtblock_pa_t_kernel(
                         out=stats[:, a, half, :],
                         in_=x_tiles[s][:, a, half * BN_MAX : (half + 1) * BN_MAX],
                     )
+            for a in tiles:
                 nc.vector.bn_aggr(
                     out=mean_var[:, a, :], in_=stats[:, a].rearrange("p h s -> p (h s)")
                 )
 
-        def scale_and_shift(s):
-            mean_var = stat_tiles[s][1]
+        def standard_deviation(s):
             std = small.tile([P, A], F32)
             nc.scalar.activation(
-                out=std[:], in_=mean_var[:, :, 1], func=ACT.Sqrt, bias=eps[:, 0:1], scale=1.0
+                out=std[:], in_=stat_tiles[s][1][:, :, 1], func=ACT.Sqrt, bias=eps[:, 0:1], scale=1.0
             )
+            stat_tiles[s] = stat_tiles[s] + (std,)
+
+        def scale_and_shift(s):
+            mean_var = stat_tiles[s][1]
+            std = stat_tiles[s][2]
             rstd = small.tile([P, A], F32)
             nc.vector.reciprocal(out=rstd[:], in_=std[:])
             shift = small.tile([P, A], F32)
@@ -162,7 +180,7 @@ def tile_swidtblock_pa_t_kernel(
                 out=shift[:], in0=mean_var[:, :, 0], scalar=-1.0, in1=rstd[:],
                 op0=ALU.mult, op1=ALU.mult,
             )
-            n_sb = work.tile([P, A, D], F32)
+            n_sb = work2.tile([P, A, D], F32)
             n_tiles[s] = (n_sb, rstd, shift)
 
         def normalise_on_gpsimd(s, tiles):
@@ -185,12 +203,12 @@ def tile_swidtblock_pa_t_kernel(
         def transpose_and_scale(s, g):
             n_sb = n_tiles[s][0]
             if s not in h_tiles:
-                h_t = work.tile([P, K_TILES, GROUP], BF16)
-                grouped = work.tile([P, PASSES, GROUP, PACK], BF16, align_bytes=64)
+                h_t = work2.tile([P, K_TILES, GROUP], BF16)
+                grouped = work3.tile([P, PASSES, GROUP, PACK], BF16, align_bytes=64)
                 h_tiles[s] = (h_t, grouped)
             h_t, grouped = h_tiles[s]
             for t in range(g * PACK, (g + 1) * PACK):
-                bank = psum_t.tile([P, GROUP], F32, tag="bank")
+                bank = psum.tile([P, BANK], F32, tag="bank")
                 for a in range(A):
                     nc.tensor.transpose(
                         bank[:, a * P : (a + 1) * P], n_sb[:, a, t * P : (t + 1) * P], ident[:]
@@ -205,34 +223,30 @@ def tile_swidtblock_pa_t_kernel(
                 scalar1=1.0, scalar2=0.0, op0=ALU.mult, op1=ALU.add,
             )
 
-        def quantise(s):
+        def quantise(s, g):
             grouped = h_tiles[s][1]
-            codes = work.tile([P, PASSES, GROUP], U32, align_bytes=64)
-            scales = work.tile([P, PASSES, GROUP], U8, align_bytes=64)
-            for g in range(PASSES):
-                nc.vector.quantize_mx(
-                    out=codes[:, g, :].bitcast(FP8X4),
-                    scales=scales[:, g, :],
-                    in_=grouped[:, g].rearrange("p c j -> p (c j)"),
-                )
-            code_tiles[s] = (codes, scales)
-
-        def project(s, tiles):
+            if s not in code_tiles:
+                codes = work3.tile([P, PASSES, GROUP], U32, align_bytes=64)
+                scales = work3.tile([P, PASSES, GROUP], U8, align_bytes=64)
+                code_tiles[s] = (codes, scales)
             codes, scales = code_tiles[s]
-            if s not in result_tiles:
-                result = opool.tile([P, 3, A, C], F32)
-                result_tiles[s] = result
-            result = result_tiles[s]
-            accs = {}
+            nc.vector.quantize_mx(
+                out=codes[:, g, :].bitcast(FP8X4),
+                scales=scales[:, g, :],
+                in_=grouped[:, g].rearrange("p c j -> p (c j)"),
+            )
+
+        def multiply(s, tiles):
+            codes, scales = code_tiles[s]
             for a in tiles:
                 tokens = slice(a * P, (a + 1) * P)
-                acc_qk = psum_o.tile([P, 2 * C], F32)
-                acc_v = psum_o.tile([P, C], F32)
-                accs[a] = (acc_qk, acc_v)
+                acc_qk = psum.tile([P, BANK], F32, tag="bank")
+                acc_v = psum.tile([P, BANK], F32, tag="bank")
+                acc_tiles[(s, a)] = (acc_qk, acc_v)
                 for g in range(PASSES):
-                    for acc, cols in ((acc_qk, QK), (acc_v, V)):
+                    for acc, cols, width in ((acc_qk, QK, 2 * C), (acc_v, V, C)):
                         nc.tensor.matmul_mx(
-                            out=acc[:],
+                            out=acc[:, 0:width],
                             lhsT=codes[:, g, tokens].bitcast(FP8X4),
                             lhsT_scale=scales[:, g, tokens],
                             rhs=w_codes[:, g, cols].bitcast(FP8X4),
@@ -240,8 +254,14 @@ def tile_swidtblock_pa_t_kernel(
                             start=(g == 0),
                             stop=(g == PASSES - 1),
                         )
+
+        def add_bias(s, tiles):
+            if s not in result_tiles:
+                result = work2.tile([P, 3, A, C], F32)
+                result_tiles[s] = result
+            result = result_tiles[s]
             for a in tiles:
-                acc_qk, acc_v = accs[a]
+                acc_qk, acc_v = acc_tiles[(s, a)]
                 nc.vector.tensor_tensor(
                     out=result[:, 0:2, a, :],
                     in0=acc_qk[:].rearrange("p (o c) -> p o c", o=2),
@@ -249,33 +269,45 @@ def tile_swidtblock_pa_t_kernel(
                     op=ALU.add,
                 )
                 nc.vector.tensor_tensor(
-                    out=result[:, 2, a, :], in0=acc_v[:], in1=out_bias[:, V], op=ALU.add
+                    out=result[:, 2, a, :], in0=acc_v[:, 0:C], in1=out_bias[:, V], op=ALU.add
                 )
 
         def store(s):
             for o in range(3):
                 nc.sync.dma_start(out=out_groups[o][s], in_=result_tiles[s][:, o])
 
+        def half_of(i):
+            return i // 2, i % 2, (2 * (i % 2), 2 * (i % 2) + 1)
+
         regroup_weights()
-        for r in range(GROUPS + 3):
-            if r == 1:
+        for u in range(STEPS + LAG_OUT):
+            if u == 2:
                 spread_vectors()
-            if r == 2:
+            if u == 3:
+                keep_spread_vectors()
+            if u == LAG_QUANTISE:
                 quantise_weights()
-            if r >= 3:
-                quantise(r - 3)
-            if 1 <= r <= GROUPS:
-                normalise_on_gpsimd(r - 1, (1, 3))
-            for half in range(2):
-                if 2 <= r <= GROUPS + 1:
-                    transpose_and_scale(r - 2, half)
-                if r < GROUPS:
-                    statistics(r, (2 * half, 2 * half + 1))
-                if r >= 3:
-                    project(r - 3, (2 * half, 2 * half + 1))
-            if r >= 3:
-                store(r - 3)
-            if 1 <= r <= GROUPS:
-                normalise_on_scalar(r - 1, (0, 2))
-            if r < GROUPS:
-                scale_and_shift(r)
+            if 0 <= u - LAG_QUANTISE < STEPS:
+                s, g, tiles = half_of(u - LAG_QUANTISE)
+                quantise(s, g)
+            if 0 <= u - LAG_TRANSPOSE < STEPS:
+                s, g, tiles = half_of(u - LAG_TRANSPOSE)
+                transpose_and_scale(s, g)
+            if 0 <= u - LAG_MULTIPLY < STEPS:
+                s, g, tiles = half_of(u - LAG_MULTIPLY)
+                multiply(s, tiles)
+            if 0 <= u - 3 < STEPS and (u - 3) % 2 == 0:
+                normalise_on_scalar((u - 3) // 2, (0, 2))
+            if 0 <= u - LAG_OUT < STEPS:
+                s, g, tiles = half_of(u - LAG_OUT)
+                add_bias(s, tiles)
+                if g == 1:
+                    store(s)
+            if u < STEPS:
+                s, g, tiles = half_of(u)
+                statistics(s, tiles)
+                if g == 1:
+                    standard_deviation(s)
+            if 0 <= u - 2 < STEPS and (u - 2) % 2 == 0:
+                scale_and_shift((u - 2) // 2)
+                normalise_on_gpsimd((u - 2) // 2, (1, 3))

from contextlib import ExitStack

import concourse.mybir as mybir
from concourse.masks import make_identity

F32 = mybir.dt.float32
BF16 = mybir.dt.bfloat16
U32 = mybir.dt.uint32
U8 = mybir.dt.uint8
FP8X4 = mybir.dt.float8_e4m3fn_x4
ALU = mybir.AluOpType
ACT = mybir.ActivationFunctionType

P = 128
PACK = 4
K_PASS = P * PACK
TOKENS = 4 * 1024
D = 1024
C = 256
EPS = 1e-6

PASSES = D // K_PASS
K_TILES = D // P
A = 4
GROUP = A * P
GROUPS = TOKENS // GROUP
BN_MAX = 512
BANK = 512
QK = slice(0, 2 * C)
V = slice(2 * C, 3 * C)

STEPS = 2 * GROUPS
LAG_TRANSPOSE = 5
LAG_QUANTISE = 8
LAG_MULTIPLY = 9
LAG_OUT = 10

FLOPS = 2 * TOKENS * D * 3 * C


def tile_swidtblock_pa_t_kernel(
    tc, x, ln1_gain, ln1_bias, wq, bq, wk, bk, wv, bv, out_0, out_1, out_2
):
    nc = tc.nc
    x_groups = x.flatten_outer_dims().rearrange("(s p a) d -> s p a d", p=P, a=A)
    out_groups = [
        o.rearrange("b t h e -> (b t) (h e)").rearrange("(s p a) c -> s p a c", p=P, a=A)
        for o in (out_0, out_1, out_2)
    ]

    with ExitStack() as ctx:
        const = ctx.enter_context(tc.tile_pool(name="const", bufs=1))
        xpool = ctx.enter_context(tc.tile_pool(name="xpool", bufs=GROUPS))
        small = ctx.enter_context(tc.tile_pool(name="small", bufs=4))
        work2 = ctx.enter_context(tc.tile_pool(name="work2", bufs=2))
        work3 = ctx.enter_context(tc.tile_pool(name="work3", bufs=3))
        psum = ctx.enter_context(tc.psum_pool(name="psum", bufs=8))
        ctx.enter_context(tc.manual_schedule())

        x_tiles = []

        def load_x(s):
            x_sb = xpool.tile([P, A, D], BF16)
            nc.sync.dma_start(out=x_sb[:], in_=x_groups[s])
            x_tiles.append(x_sb)

        load_x(0)
        w_raw = const.tile([P, 3, PASSES, PACK, C], BF16)
        for o, w in enumerate((wq, wk, wv)):
            nc.sync.dma_start(
                out=w_raw[:, o], in_=w.rearrange("(g j p) c -> p g j c", j=PACK, p=P)
            )
        for s in range(1, GROUPS):
            load_x(s)

        ident = const.tile([P, P], F32)
        make_identity(nc, ident[:])
        eps = const.tile([P, 1], F32)
        nc.vector.memset(eps[:], EPS)
        ones = const.tile([P, P], BF16)
        nc.vector.memset(ones[:], 1.0)

        ln_rows = const.tile([P, P], BF16)
        nc.vector.memset(ln_rows[:], 0.0)
        nc.scalar.dma_start(out=ln_rows[0:K_TILES, :], in_=ln1_gain.rearrange("(r c) -> r c", c=P))
        nc.scalar.dma_start(
            out=ln_rows[K_TILES : 2 * K_TILES, :], in_=ln1_bias.rearrange("(r c) -> r c", c=P)
        )
        bias_rows = const.tile([P, 3 * C], BF16)
        nc.vector.memset(bias_rows[:], 0.0)
        for o, b in enumerate((bq, bk, bv)):
            nc.scalar.dma_start(
                out=bias_rows[0:1, o * C : (o + 1) * C], in_=b.rearrange("(r c) -> r c", r=1)
            )
        ln_cols = const.tile([P, 2 * K_TILES], F32)
        out_bias = const.tile([P, 3 * C], F32)
        spread = {}

        def spread_vectors():
            ln_rows_f32 = const.tile([P, P], F32)
            nc.vector.tensor_copy(out=ln_rows_f32[:], in_=ln_rows[:])
            ln_cols_ps = psum.tile([P, BANK], F32, tag="bank")
            nc.tensor.transpose(ln_cols_ps[:, 0:P], ln_rows_f32[:], ident[:])
            spread["ln"] = ln_cols_ps
            for name, cols, width in (("qk", QK, 2 * C), ("v", V, C)):
                bias_ps = psum.tile([P, BANK], F32, tag="bank")
                nc.tensor.matmul(
                    bias_ps[:, 0:width], lhsT=ones[:], rhs=bias_rows[:, cols], start=True, stop=True
                )
                spread[name] = bias_ps

        def keep_spread_vectors():
            nc.vector.tensor_copy(out=ln_cols[:], in_=spread["ln"][:, 0 : 2 * K_TILES])
            nc.vector.tensor_copy(out=out_bias[:, QK], in_=spread["qk"][:, 0 : 2 * C])
            nc.vector.tensor_copy(out=out_bias[:, V], in_=spread["v"][:, 0:C])

        w_grouped = const.tile([P, PASSES, 3 * C, PACK], BF16, align_bytes=64)
        w_codes = const.tile([P, PASSES, 3 * C], U32, align_bytes=64)
        w_scales = const.tile([P, PASSES, 3 * C], U8, align_bytes=64)

        def regroup_weights():
            for o in range(3):
                for g in range(PASSES):
                    dst = w_grouped[:, g, o * C : (o + 1) * C, :]
                    src = w_raw[:, o, g].rearrange("p j c -> p c j")
                    if g % 2 == 0:
                        nc.scalar.copy(out=dst, in_=src)
                    else:
                        nc.gpsimd.tensor_scalar(
                            out=dst, in0=src, scalar1=1.0, scalar2=0.0, op0=ALU.mult, op1=ALU.add
                        )

        def quantise_weights():
            for g in range(PASSES):
                for cols in (QK, V):
                    nc.vector.quantize_mx(
                        out=w_codes[:, g, cols].bitcast(FP8X4),
                        scales=w_scales[:, g, cols],
                        in_=w_grouped[:, g, cols, :].rearrange("p c j -> p (c j)"),
                    )

        stat_tiles = {}
        n_tiles = {}
        h_tiles = {}
        code_tiles = {}
        acc_tiles = {}
        result_tiles = {}

        def statistics(s, tiles):
            if s not in stat_tiles:
                stats = small.tile([P, A, D // BN_MAX, 6], F32)
                mean_var = small.tile([P, A, 2], F32)
                stat_tiles[s] = (stats, mean_var)
            stats, mean_var = stat_tiles[s]
            for a in tiles:
                for half in range(D // BN_MAX):
                    nc.vector.bn_stats(
                        out=stats[:, a, half, :],
                        in_=x_tiles[s][:, a, half * BN_MAX : (half + 1) * BN_MAX],
                    )
            for a in tiles:
                nc.vector.bn_aggr(
                    out=mean_var[:, a, :], in_=stats[:, a].rearrange("p h s -> p (h s)")
                )

        def standard_deviation(s):
            std = small.tile([P, A], F32)
            nc.scalar.activation(
                out=std[:], in_=stat_tiles[s][1][:, :, 1], func=ACT.Sqrt, bias=eps[:, 0:1], scale=1.0
            )
            stat_tiles[s] = stat_tiles[s] + (std,)

        def scale_and_shift(s):
            mean_var = stat_tiles[s][1]
            std = stat_tiles[s][2]
            rstd = small.tile([P, A], F32)
            nc.vector.reciprocal(out=rstd[:], in_=std[:])
            shift = small.tile([P, A], F32)
            nc.vector.scalar_tensor_tensor(
                out=shift[:], in0=mean_var[:, :, 0], scalar=-1.0, in1=rstd[:],
                op0=ALU.mult, op1=ALU.mult,
            )
            n_sb = work2.tile([P, A, D], F32)
            n_tiles[s] = (n_sb, rstd, shift)

        def normalise_on_gpsimd(s, tiles):
            n_sb, rstd, shift = n_tiles[s]
            for a in tiles:
                nc.gpsimd.tensor_scalar(
                    out=n_sb[:, a, :], in0=x_tiles[s][:, a, :],
                    scalar1=rstd[:, a : a + 1], scalar2=shift[:, a : a + 1],
                    op0=ALU.mult, op1=ALU.add,
                )

        def normalise_on_scalar(s, tiles):
            n_sb, rstd, shift = n_tiles[s]
            for a in tiles:
                nc.scalar.activation(
                    out=n_sb[:, a, :], in_=x_tiles[s][:, a, :], func=ACT.Identity,
                    scale=rstd[:, a : a + 1], bias=shift[:, a : a + 1],
                )

        def transpose_and_scale(s, g):
            n_sb = n_tiles[s][0]
            if s not in h_tiles:
                h_t = work2.tile([P, K_TILES, GROUP], BF16)
                grouped = work3.tile([P, PASSES, GROUP, PACK], BF16, align_bytes=64)
                h_tiles[s] = (h_t, grouped)
            h_t, grouped = h_tiles[s]
            for t in range(g * PACK, (g + 1) * PACK):
                bank = psum.tile([P, BANK], F32, tag="bank")
                for a in range(A):
                    nc.tensor.transpose(
                        bank[:, a * P : (a + 1) * P], n_sb[:, a, t * P : (t + 1) * P], ident[:]
                    )
                nc.scalar.activation(
                    out=h_t[:, t, :], in_=bank[:], func=ACT.Identity,
                    scale=ln_cols[:, t : t + 1], bias=ln_cols[:, K_TILES + t : K_TILES + t + 1],
                )
            nc.gpsimd.tensor_scalar(
                out=grouped[:, g],
                in0=h_t[:, g * PACK : (g + 1) * PACK, :].rearrange("p j c -> p c j"),
                scalar1=1.0, scalar2=0.0, op0=ALU.mult, op1=ALU.add,
            )

        def quantise(s, g):
            grouped = h_tiles[s][1]
            if s not in code_tiles:
                codes = work3.tile([P, PASSES, GROUP], U32, align_bytes=64)
                scales = work3.tile([P, PASSES, GROUP], U8, align_bytes=64)
                code_tiles[s] = (codes, scales)
            codes, scales = code_tiles[s]
            nc.vector.quantize_mx(
                out=codes[:, g, :].bitcast(FP8X4),
                scales=scales[:, g, :],
                in_=grouped[:, g].rearrange("p c j -> p (c j)"),
            )

        def multiply(s, tiles):
            codes, scales = code_tiles[s]
            for a in tiles:
                tokens = slice(a * P, (a + 1) * P)
                acc_qk = psum.tile([P, BANK], F32, tag="bank")
                acc_v = psum.tile([P, BANK], F32, tag="bank")
                acc_tiles[(s, a)] = (acc_qk, acc_v)
                for g in range(PASSES):
                    for acc, cols, width in ((acc_qk, QK, 2 * C), (acc_v, V, C)):
                        nc.tensor.matmul_mx(
                            out=acc[:, 0:width],
                            lhsT=codes[:, g, tokens].bitcast(FP8X4),
                            lhsT_scale=scales[:, g, tokens],
                            rhs=w_codes[:, g, cols].bitcast(FP8X4),
                            rhs_scale=w_scales[:, g, cols],
                            start=(g == 0),
                            stop=(g == PASSES - 1),
                        )

        def add_bias(s, tiles):
            if s not in result_tiles:
                result = work2.tile([P, 3, A, C], F32)
                result_tiles[s] = result
            result = result_tiles[s]
            for a in tiles:
                acc_qk, acc_v = acc_tiles[(s, a)]
                nc.vector.tensor_tensor(
                    out=result[:, 0:2, a, :],
                    in0=acc_qk[:].rearrange("p (o c) -> p o c", o=2),
                    in1=out_bias[:, QK].rearrange("p (o c) -> p o c", o=2),
                    op=ALU.add,
                )
                nc.vector.tensor_tensor(
                    out=result[:, 2, a, :], in0=acc_v[:, 0:C], in1=out_bias[:, V], op=ALU.add
                )

        def store(s):
            for o in range(3):
                nc.sync.dma_start(out=out_groups[o][s], in_=result_tiles[s][:, o])

        def half_of(i):
            return i // 2, i % 2, (2 * (i % 2), 2 * (i % 2) + 1)

        regroup_weights()
        for u in range(STEPS + LAG_OUT):
            if u == 2:
                spread_vectors()
            if u == 3:
                keep_spread_vectors()
            if u == LAG_QUANTISE:
                quantise_weights()
            if 0 <= u - LAG_QUANTISE < STEPS:
                s, g, tiles = half_of(u - LAG_QUANTISE)
                quantise(s, g)
            if 0 <= u - LAG_TRANSPOSE < STEPS:
                s, g, tiles = half_of(u - LAG_TRANSPOSE)
                transpose_and_scale(s, g)
            if 0 <= u - LAG_MULTIPLY < STEPS:
                s, g, tiles = half_of(u - LAG_MULTIPLY)
                multiply(s, tiles)
            if 0 <= u - 3 < STEPS and (u - 3) % 2 == 0:
                normalise_on_scalar((u - 3) // 2, (0, 2))
            if 0 <= u - LAG_OUT < STEPS:
                s, g, tiles = half_of(u - LAG_OUT)
                add_bias(s, tiles)
                if g == 1:
                    store(s)
            if u < STEPS:
                s, g, tiles = half_of(u)
                statistics(s, tiles)
                if g == 1:
                    standard_deviation(s)
            if 0 <= u - 2 < STEPS and (u - 2) % 2 == 0:
                scale_and_shift((u - 2) // 2)
                normalise_on_gpsimd((u - 2) // 2, (1, 3))
